import numpy as np
import ml_dtypes


def mxq(x, axis, fmt="e4m3"):
    dtype, down = {"e4m3": (ml_dtypes.float8_e4m3fn, 7), "e5m2": (ml_dtypes.float8_e5m2, 14)}[fmt]
    v = np.moveaxis(np.asarray(x, np.float32).astype(ml_dtypes.bfloat16).astype(np.float64), axis, -1)
    blocks = v.reshape(v.shape[:-1] + (-1, 32))
    amax = np.abs(blocks).max(-1, keepdims=True)
    byte = np.maximum(np.where(amax > 0, np.frexp(amax)[1] - 1 + 127, 0) - down, 1)
    scale = np.exp2(byte - 127.0)
    codes = (blocks / scale).astype(np.float32).astype(dtype).astype(np.float64)
    return np.moveaxis((codes * scale).reshape(v.shape), -1, axis)


WIDE = False


def mx_kscale(k):
    if not WIDE:
        return np.ones(k)
    levels = np.array([10, -10, 5, -5, 0])
    a = np.random.permutation(np.resize(levels, k // 512 * 4)).reshape(k // 512, 4)
    idx = np.arange(k)
    return np.exp2(a[idx // 512, idx % 128 // 32])


BF16 = ml_dtypes.bfloat16


def bf(x):
    return np.asarray(x, np.float32).astype(BF16)


def f64(x):
    return np.asarray(x).astype(np.float64)


B, Q_LEN, CTX, HID, H, KVH, D = 4, 128, 1408, 1024, 4, 2, 128
T = CTX + Q_LEN
EPS = 1e-6
ROPE_BASE = 10000.0


def rms_norm(x, w):
    return x * (1.0 / np.sqrt(np.mean(x * x, axis=-1, keepdims=True) + EPS)) * w


def rotate_half(x):
    h = x.shape[-1] // 2
    return np.concatenate([-x[..., h:], x[..., :h]], axis=-1)


def setup_inputs():
    s = mx_kscale(HID)
    inv_freq = 1.0 / ROPE_BASE ** (np.arange(0, D, 2) / D)
    pos = np.random.randint(0, CTX, size=(B, 1)) + np.arange(T)[None, :]
    ang = pos[:, :, None] * inv_freq
    emb = np.concatenate([ang, ang], axis=-1)
    return {"hidden_states": bf(np.random.standard_normal((B, Q_LEN, HID)) * s),
            "target_hidden": bf(np.random.standard_normal((B, CTX, HID)) * s),
            "cos": bf(np.cos(emb)),
            "sin": bf(np.sin(emb)),
            "Wq": bf(np.random.standard_normal((H * D, HID)) / np.sqrt(HID) / s[None, :]),
            "Wk": bf(np.random.standard_normal((KVH * D, HID)) / np.sqrt(HID) / s[None, :]),
            "Wv": bf(np.random.standard_normal((KVH * D, HID)) * 2.0 / np.sqrt(HID) / s[None, :]),
            "q_norm_w": bf(1.0 + 0.1 * np.random.standard_normal(D)),
            "k_norm_w": bf(1.0 + 0.1 * np.random.standard_normal(D))}


def reference(hidden_states, target_hidden, cos, sin, Wq, Wk, Wv, q_norm_w, k_norm_w):
    kv_in = mxq(np.concatenate([f64(target_hidden), f64(hidden_states)], axis=1), 2, "e4m3")
    h_in = kv_in[:, CTX:, :]
    q = (h_in @ mxq(f64(Wq), 1, "e4m3").T).reshape(B, Q_LEN, H, D)
    q = rms_norm(q, f64(q_norm_w)).transpose(0, 2, 1, 3)
    k = (kv_in @ mxq(f64(Wk), 1, "e4m3").T).reshape(B, T, KVH, D)
    k = rms_norm(k, f64(k_norm_w)).transpose(0, 2, 1, 3)
    v = (kv_in @ mxq(f64(Wv), 1, "e4m3").T).reshape(B, T, KVH, D).transpose(0, 2, 1, 3)
    c = f64(cos)[:, None, :, :]
    s = f64(sin)[:, None, :, :]
    q = q * c[:, :, -Q_LEN:, :] + rotate_half(q) * s[:, :, -Q_LEN:, :]
    k = k * c + rotate_half(k) * s
    return q, k, v

@@ -1,0 +1,278 @@
+from contextlib import ExitStack
+
+import concourse.mybir as mybir
+from concourse.masks import make_identity
+
+FP8X4 = mybir.dt.float8_e4m3fn_x4
+BF16 = mybir.dt.bfloat16
+F32 = mybir.dt.float32
+U32 = mybir.dt.uint32
+U8 = mybir.dt.uint8
+ACT = mybir.ActivationFunctionType
+ALU = mybir.AluOpType
+
+P = 128
+B, Q_LEN, CTX, HID, H, KVH, D = 4, 128, 1408, 1024, 4, 2, 128
+T = CTX + Q_LEN
+EPS = 1e-6
+HALF = D // 2
+
+FLOPS = 2 * HID * (B * T * 2 * KVH * D + B * Q_LEN * H * D)
+
+K_PASS = 512
+PASSES = HID // K_PASS
+ROW_WORDS = HID // 2
+ROW_CODES = HID // 4
+N_OUT = 512
+
+CTX_ROWS = CTX // P
+TILES = CTX_ROWS + 1
+CHUNK = 4
+CHUNKS = TILES // CHUNK
+RUN = 2
+N_CHUNKS = B * CHUNKS
+ROUNDS_PER_CHUNK = CHUNK // RUN
+N_ROUNDS = N_CHUNKS * ROUNDS_PER_CHUNK
+PREFETCH = 5
+
+
+def tile_dflashattention_pa_t_kernel(
+    tc, hidden_states, target_hidden, cos, sin, Wq, Wk, Wv, q_norm_w, k_norm_w, out_q, out_k, out_v
+):
+    nc = tc.nc
+    with ExitStack() as stack:
+        const = stack.enter_context(tc.tile_pool(name="const", bufs=1))
+        x_pool = stack.enter_context(tc.tile_pool(name="x", bufs=PREFETCH + 1))
+        angle_pool = stack.enter_context(tc.tile_pool(name="angles", bufs=2))
+        table_pool = stack.enter_context(tc.tile_pool(name="tables", bufs=3))
+        quant_pool = stack.enter_context(tc.tile_pool(name="quant", bufs=3))
+        stat_pool = stack.enter_context(tc.tile_pool(name="stats", bufs=3 * RUN))
+        prod_pool = stack.enter_context(tc.tile_pool(name="products", bufs=2))
+        out_pool = stack.enter_context(tc.tile_pool(name="staged", bufs=3))
+        flip_psum = stack.enter_context(tc.psum_pool(name="flip", bufs=3))
+        kv_psum = stack.enter_context(tc.psum_pool(name="kv", bufs=2 * RUN))
+        q_psum = stack.enter_context(tc.psum_pool(name="q", bufs=1))
+        stack.enter_context(tc.manual_schedule())
+
+        identity = const.tile([P, P], F32)
+        make_identity(nc, identity[:])
+        one = const.tile([P, 1], F32)
+        nc.vector.memset(one[:], 1.0)
+        warm = const.tile([P, 1], F32)
+        nc.scalar.activation(out=warm[:], in_=one[:], func=ACT.Abs_reciprocal_sqrt)
+        wk_rows = const.tile([P, D], BF16)
+        nc.scalar.dma_start(out=wk_rows[:], in_=k_norm_w.partition_broadcast(P))
+        wq_rows = const.tile([P, D], BF16)
+        nc.scalar.dma_start(out=wq_rows[:], in_=q_norm_w.partition_broadcast(P))
+
+        def flip_rows(words):
+            flipped = flip_psum.tile([P, PASSES, 2, P], F32)
+            for g in range(PASSES):
+                for u in range(2):
+                    first = (2 * g + u) * P
+                    nc.tensor.transpose(flipped[:, g, u, :], words[:, first : first + P], identity[:])
+            return flipped
+
+        def copy_grouped(copy, grouped_words, flipped):
+            copy(out=grouped_words, in_=flipped[:].rearrange("p g u r -> p g r u"))
+
+        def load_chunk(n):
+            b, c = divmod(n, CHUNKS)
+            x_sb = x_pool.tile([P, CHUNK * HID], BF16)
+            local, first, last = context_range(c)
+            if c == 0:
+                nc.sync.dma_start(out=x_sb[:, 0:HID], in_=hidden_states[b])
+            rows = target_hidden[b].rearrange("(p j) c -> p (j c)", j=CTX_ROWS)
+            nc.sync.dma_start(out=x_sb[:, local * HID :], in_=rows[:, first * HID : last * HID])
+            return x_sb
+
+        def load_angles(table, b, tag):
+            angle_sb = angle_pool.tile([P, TILES, D], BF16, name=tag)
+            nc.sync.dma_start(out=angle_sb[:, 0, :], in_=table[b, CTX:T, :])
+            nc.sync.dma_start(
+                out=angle_sb[:, 1:TILES, :], in_=table[b, 0:CTX, :].rearrange("(p j) d -> p j d", j=CTX_ROWS)
+            )
+            return angle_sb
+
+        def rope_table(cos_sb, sin_sb, first, count, w_rows, tag):
+            table = table_pool.tile([P, count, 2, D], F32, name="table", tag=tag)
+            tiles = slice(first, first + count)
+            low, high = slice(0, HALF), slice(HALF, D)
+
+            def weighted(out, angle, w):
+                nc.gpsimd.tensor_tensor(out=out, in0=angle, in1=w.unsqueeze(1).to_broadcast(out.shape), op=ALU.mult)
+
+            weighted(table[:, :, 0, :], cos_sb[:, tiles, :], w_rows[:])
+            weighted(table[:, :, 1, low], sin_sb[:, tiles, high], w_rows[:, low])
+            weighted(table[:, :, 1, high], sin_sb[:, tiles, low], w_rows[:, high])
+            return table
+
+        def sum_squares(product, heads, tag):
+            sumsq = stat_pool.tile([P, heads], F32, name="sumsq", tag="sumsq" + tag)
+            squares = stat_pool.tile([P, heads * D], BF16, name="squares", tag="squares" + tag)
+            for h in range(heads):
+                cols = slice(h * D, (h + 1) * D)
+                nc.scalar.activation(
+                    out=squares[:, cols], in_=product[:, cols], func=ACT.Square, accum_out=sumsq[:, h : h + 1]
+                )
+            return sumsq
+
+        def inverse_rms(sumsq, heads, tag):
+            rstd = stat_pool.tile([P, heads], F32, name="rstd", tag="rstd" + tag)
+            nc.scalar.activation(out=rstd[:], in_=sumsq[:], func=ACT.Abs_reciprocal_sqrt, scale=1.0 / D, bias=EPS)
+            return rstd
+
+        def table_products(terms, product, h, rstd, table):
+            nc.vector.scalar_tensor_tensor(
+                out=terms,
+                in0=product[:, h * D : (h + 1) * D].unsqueeze(1).to_broadcast([P, 2, D]),
+                scalar=rstd[:, h : h + 1],
+                in1=table,
+                op0=ALU.mult,
+                op1=ALU.mult,
+            )
+
+        def add_swapped(staged, terms):
+            nc.vector.tensor_tensor(
+                out=staged[:, :, :, 0:HALF], in0=terms[:, :, :, 0, 0:HALF], in1=terms[:, :, :, 1, HALF:D],
+                op=ALU.subtract,
+            )
+            nc.vector.tensor_tensor(
+                out=staged[:, :, :, HALF:D], in0=terms[:, :, :, 0, HALF:D], in1=terms[:, :, :, 1, 0:HALF],
+                op=ALU.add,
+            )
+
+        def store_chunk(dst, staged, n):
+            b, c = divmod(n, CHUNKS)
+            local, first, last = context_range(c)
+            rows = dst[b, :, 0:CTX, :].rearrange("h (p j) d -> p h j d", j=CTX_ROWS)
+            nc.sync.dma_start(out=rows[:, :, first:last, :], in_=staged[:, :, local:CHUNK, :])
+            if c == 0:
+                nc.sync.dma_start(out=dst[b, :, CTX:T, :].rearrange("h p d -> p h d"), in_=staged[:, :, 0, :])
+
+        w_heads = [Wk[0:P, :], Wk[P : 2 * P, :], Wv[0:P, :], Wv[P : 2 * P, :]]
+        w_heads.extend(Wq[h * P : (h + 1) * P, :] for h in range(H))
+        w_raw = const.tile([P, len(w_heads) * HID], BF16)
+        for i, rows in enumerate(w_heads):
+            nc.sync.dma_start(out=w_raw[:, i * HID : (i + 1) * HID], in_=rows)
+
+        x_chunks = {}
+        for n in range(PREFETCH):
+            x_chunks[n] = load_chunk(n)
+            if n == 0:
+                angles = {0: (load_angles(cos, 0, "cos_sb"), load_angles(sin, 0, "sin_sb"))}
+
+        w_codes, w_scales = {}, {}
+        for block, name in enumerate(("kv", "q")):
+            w_grouped = const.tile([P, PASSES * N_OUT * 4], BF16, name="w_grouped_" + name, align_bytes=64)
+            grouped_words = w_grouped[:].bitcast(F32).rearrange("p (g n u) -> p g n u", g=PASSES, u=2)
+            for i in range(N_OUT // P):
+                head = block * (N_OUT // P) + i
+                flipped = flip_rows(w_raw[:, head * HID : (head + 1) * HID].bitcast(F32))
+                copy = nc.scalar.copy if i % 2 == 0 else nc.vector.tensor_copy
+                copy_grouped(copy, grouped_words[:, :, i * P : (i + 1) * P, :], flipped)
+            w_codes[name] = const.tile([P, PASSES * N_OUT], U32, name="w_codes_" + name, align_bytes=64)
+            w_scales[name] = const.tile([P, PASSES * N_OUT], U8, name="w_scales_" + name, align_bytes=64)
+            nc.vector.quantize_mx(out=w_codes[name][:].bitcast(FP8X4), scales=w_scales[name][:], in_=w_grouped[:])
+
+        grouped, codes, scales = {}, {}, {}
+        products, rstds = {}, {}
+        tables, q_tables, k_staged, v_staged = {}, {}, {}, {}
+
+        def project(out, r, t, name):
+            for g in range(PASSES):
+                x_cols = slice(t * ROW_CODES + g * P, t * ROW_CODES + (g + 1) * P)
+                w_cols = slice(g * N_OUT, (g + 1) * N_OUT)
+                nc.tensor.matmul_mx(
+                    out=out,
+                    lhsT=codes[r][:, x_cols].bitcast(FP8X4),
+                    lhsT_scale=scales[r][:, x_cols],
+                    rhs=w_codes[name][:, w_cols].bitcast(FP8X4),
+                    rhs_scale=w_scales[name][:, w_cols],
+                    start=(g == 0),
+                    stop=(g == PASSES - 1),
+                )
+
+        def flip_round(r):
+            n, part = divmod(r, ROUNDS_PER_CHUNK)
+            b, c = divmod(n, CHUNKS)
+            if part == 0:
+                if n + PREFETCH < N_CHUNKS:
+                    x_chunks[n + PREFETCH] = load_chunk(n + PREFETCH)
+                if c == 0 and b + 1 < B:
+                    angles[b + 1] = (load_angles(cos, b + 1, "cos_sb"), load_angles(sin, b + 1, "sin_sb"))
+                cos_sb, sin_sb = angles[b]
+                if c == 0:
+                    q_tables[b] = rope_table(cos_sb, sin_sb, 0, 1, wq_rows, "q")
+                tables[n] = rope_table(cos_sb, sin_sb, c * CHUNK, CHUNK, wk_rows, "k")
+            grouped[r] = quant_pool.tile([P, RUN * HID], BF16, name="grouped", align_bytes=64)
+            words = x_chunks[n][:].bitcast(F32)
+            flipped = [
+                flip_rows(words[:, (part * RUN + t) * ROW_WORDS : (part * RUN + t + 1) * ROW_WORDS])
+                for t in range(RUN)
+            ]
+            for t in range(RUN):
+                tile_words = grouped[r][:, t * HID : (t + 1) * HID].bitcast(F32)
+                copy_grouped(nc.scalar.copy, tile_words.rearrange("p (g r u) -> p g r u", g=PASSES, u=2), flipped[t])
+
+        def quantise_round(r):
+            codes[r] = quant_pool.tile([P, RUN * ROW_CODES], U32, name="codes", align_bytes=64)
+            scales[r] = quant_pool.tile([P, RUN * ROW_CODES], U8, name="scales", align_bytes=64)
+            nc.vector.quantize_mx(out=codes[r][:].bitcast(FP8X4), scales=scales[r][:], in_=grouped[r][:])
+
+        def project_round(r):
+            n, part = divmod(r, ROUNDS_PER_CHUNK)
+            has_q = r % (CHUNKS * ROUNDS_PER_CHUNK) == 0
+            if part == 0:
+                k_staged[n] = out_pool.tile([P, KVH, CHUNK, D], F32, name="k_staged")
+                v_staged[n] = out_pool.tile([P, KVH, CHUNK, D], F32, name="v_staged")
+            for t in range(RUN):
+                products[r, t] = kv_psum.tile([P, N_OUT], F32, name="kv_product")
+                project(products[r, t][:], r, t, "kv")
+                if has_q and t == 0:
+                    products[r, "q"] = q_psum.tile([P, N_OUT], F32, name="q_product")
+                    project(products[r, "q"][:], r, t, "q")
+            for t in range(RUN):
+                k_sumsq = sum_squares(products[r, t], KVH, "k")
+                if has_q and t == 0:
+                    q_sumsq = sum_squares(products[r, "q"], H, "q")
+                nc.scalar.copy(
+                    out=v_staged[n][:, :, part * RUN + t, :],
+                    in_=products[r, t][:, KVH * D :].rearrange("p (h d) -> p h d", h=KVH),
+                )
+                rstds[r, t] = inverse_rms(k_sumsq, KVH, "k")
+                if has_q and t == 0:
+                    rstds[r, "q"] = inverse_rms(q_sumsq, H, "q")
+            if part == ROUNDS_PER_CHUNK - 1:
+                store_chunk(out_v, v_staged[n], n)
+
+        def rotate_round(r):
+            n, part = divmod(r, ROUNDS_PER_CHUNK)
+            b = n // CHUNKS
+            has_q = r % (CHUNKS * ROUNDS_PER_CHUNK) == 0
+            k_terms = prod_pool.tile([P, KVH, RUN, 2, D], F32)
+            for t in range(RUN):
+                for h in range(KVH):
+                    table_products(k_terms[:, h, t, :, :], products[r, t], h, rstds[r, t], tables[n][:, part * RUN + t, :, :])
+            add_swapped(k_staged[n][:, :, part * RUN : (part + 1) * RUN, :], k_terms)
+            if part == ROUNDS_PER_CHUNK - 1:
+                store_chunk(out_k, k_staged[n], n)
+            if has_q:
+                q_terms = prod_pool.tile([P, H, 1, 2, D], F32)
+                for h in range(H):
+                    table_products(q_terms[:, h, 0, :, :], products[r, "q"], h, rstds[r, "q"], q_tables[b][:, 0, :, :])
+                q_staged = out_pool.tile([P, H, 1, D], F32)
+                add_swapped(q_staged, q_terms)
+                nc.sync.dma_start(out=out_q[b].rearrange("h p d -> p h d"), in_=q_staged[:, :, 0, :])
+
+        stages = (flip_round, quantise_round, project_round, rotate_round)
+        for step in range(N_ROUNDS + len(stages) - 1):
+            for lag, stage in enumerate(stages):
+                if 0 <= step - lag < N_ROUNDS:
+                    stage(step - lag)
+
+
+def context_range(c):
+    local = 1 if c == 0 else 0
+    first = c * CHUNK + local - 1
+    return local, first, c * CHUNK + CHUNK - 1

@@ -34,6 +34,7 @@ N_CHUNKS = B * CHUNKS
 ROUNDS_PER_CHUNK = CHUNK // RUN
 N_ROUNDS = N_CHUNKS * ROUNDS_PER_CHUNK
 PREFETCH = 5
+AHEAD = 2
 
 
 def tile_dflashattention_pa_t_kernel(
@@ -44,7 +45,7 @@ def tile_dflashattention_pa_t_kernel(
         const = stack.enter_context(tc.tile_pool(name="const", bufs=1))
         x_pool = stack.enter_context(tc.tile_pool(name="x", bufs=PREFETCH + 1))
         angle_pool = stack.enter_context(tc.tile_pool(name="angles", bufs=2))
-        table_pool = stack.enter_context(tc.tile_pool(name="tables", bufs=3))
+        table_pool = stack.enter_context(tc.tile_pool(name="tables", bufs=AHEAD + 2))
         quant_pool = stack.enter_context(tc.tile_pool(name="quant", bufs=3))
         stat_pool = stack.enter_context(tc.tile_pool(name="stats", bufs=3 * RUN))
         prod_pool = stack.enter_context(tc.tile_pool(name="products", bufs=2))
@@ -100,7 +101,7 @@ def tile_dflashattention_pa_t_kernel(
             low, high = slice(0, HALF), slice(HALF, D)
 
             def weighted(out, angle, w):
-                nc.gpsimd.tensor_tensor(out=out, in0=angle, in1=w.unsqueeze(1).to_broadcast(out.shape), op=ALU.mult)
+                nc.vector.tensor_tensor(out=out, in0=angle, in1=w.unsqueeze(1).to_broadcast(out.shape), op=ALU.mult)
 
             weighted(table[:, :, 0, :], cos_sb[:, tiles, :], w_rows[:])
             weighted(table[:, :, 1, low], sin_sb[:, tiles, high], w_rows[:, low])
@@ -152,15 +153,25 @@ def tile_dflashattention_pa_t_kernel(
 
         w_heads = [Wk[0:P, :], Wk[P : 2 * P, :], Wv[0:P, :], Wv[P : 2 * P, :]]
         w_heads.extend(Wq[h * P : (h + 1) * P, :] for h in range(H))
+        angles = {0: (load_angles(cos, 0, "cos_sb"), load_angles(sin, 0, "sin_sb"))}
         w_raw = const.tile([P, len(w_heads) * HID], BF16)
         for i, rows in enumerate(w_heads):
             nc.sync.dma_start(out=w_raw[:, i * HID : (i + 1) * HID], in_=rows)
-
         x_chunks = {}
         for n in range(PREFETCH):
             x_chunks[n] = load_chunk(n)
-            if n == 0:
-                angles = {0: (load_angles(cos, 0, "cos_sb"), load_angles(sin, 0, "sin_sb"))}
+
+        tables, q_tables = {}, {}
+
+        def build_tables(n):
+            b, c = divmod(n, CHUNKS)
+            cos_sb, sin_sb = angles[b]
+            tables[n] = rope_table(cos_sb, sin_sb, c * CHUNK, CHUNK, wk_rows, "k")
+            if c == 0:
+                q_tables[b] = rope_table(cos_sb, sin_sb, 0, 1, wq_rows, "q")
+
+        for n in range(AHEAD):
+            build_tables(n)
 
         w_codes, w_scales = {}, {}
         for block, name in enumerate(("kv", "q")):
@@ -169,15 +180,14 @@ def tile_dflashattention_pa_t_kernel(
             for i in range(N_OUT // P):
                 head = block * (N_OUT // P) + i
                 flipped = flip_rows(w_raw[:, head * HID : (head + 1) * HID].bitcast(F32))
-                copy = nc.scalar.copy if i % 2 == 0 else nc.vector.tensor_copy
-                copy_grouped(copy, grouped_words[:, :, i * P : (i + 1) * P, :], flipped)
+                copy_grouped(nc.scalar.copy, grouped_words[:, :, i * P : (i + 1) * P, :], flipped)
             w_codes[name] = const.tile([P, PASSES * N_OUT], U32, name="w_codes_" + name, align_bytes=64)
             w_scales[name] = const.tile([P, PASSES * N_OUT], U8, name="w_scales_" + name, align_bytes=64)
             nc.vector.quantize_mx(out=w_codes[name][:].bitcast(FP8X4), scales=w_scales[name][:], in_=w_grouped[:])
 
-        grouped, codes, scales = {}, {}, {}
+        grouped, codes, scales, k_terms, q_terms = {}, {}, {}, {}, {}
         products, rstds = {}, {}
-        tables, q_tables, k_staged, v_staged = {}, {}, {}, {}
+        k_staged, v_staged = {}, {}
 
         def project(out, r, t, name):
             for g in range(PASSES):
@@ -195,16 +205,6 @@ def tile_dflashattention_pa_t_kernel(
 
         def flip_round(r):
             n, part = divmod(r, ROUNDS_PER_CHUNK)
-            b, c = divmod(n, CHUNKS)
-            if part == 0:
-                if n + PREFETCH < N_CHUNKS:
-                    x_chunks[n + PREFETCH] = load_chunk(n + PREFETCH)
-                if c == 0 and b + 1 < B:
-                    angles[b + 1] = (load_angles(cos, b + 1, "cos_sb"), load_angles(sin, b + 1, "sin_sb"))
-                cos_sb, sin_sb = angles[b]
-                if c == 0:
-                    q_tables[b] = rope_table(cos_sb, sin_sb, 0, 1, wq_rows, "q")
-                tables[n] = rope_table(cos_sb, sin_sb, c * CHUNK, CHUNK, wk_rows, "k")
             grouped[r] = quant_pool.tile([P, RUN * HID], BF16, name="grouped", align_bytes=64)
             words = x_chunks[n][:].bitcast(F32)
             flipped = [
@@ -246,30 +246,43 @@ def tile_dflashattention_pa_t_kernel(
             if part == ROUNDS_PER_CHUNK - 1:
                 store_chunk(out_v, v_staged[n], n)
 
-        def rotate_round(r):
+        def multiply_round(r):
             n, part = divmod(r, ROUNDS_PER_CHUNK)
-            b = n // CHUNKS
-            has_q = r % (CHUNKS * ROUNDS_PER_CHUNK) == 0
-            k_terms = prod_pool.tile([P, KVH, RUN, 2, D], F32)
+            k_terms[r] = prod_pool.tile([P, KVH, RUN, 2, D], F32, name="k_terms")
             for t in range(RUN):
                 for h in range(KVH):
-                    table_products(k_terms[:, h, t, :, :], products[r, t], h, rstds[r, t], tables[n][:, part * RUN + t, :, :])
-            add_swapped(k_staged[n][:, :, part * RUN : (part + 1) * RUN, :], k_terms)
+                    table_products(k_terms[r][:, h, t, :, :], products[r, t], h, rstds[r, t], tables[n][:, part * RUN + t, :, :])
+            if r % (CHUNKS * ROUNDS_PER_CHUNK) == 0:
+                q_terms[r] = prod_pool.tile([P, H, 1, 2, D], F32, name="q_terms")
+                for h in range(H):
+                    table_products(q_terms[r][:, h, 0, :, :], products[r, "q"], h, rstds[r, "q"], q_tables[n // CHUNKS][:, 0, :, :])
+
+        def add_round(r):
+            n, part = divmod(r, ROUNDS_PER_CHUNK)
+            add_swapped(k_staged[n][:, :, part * RUN : (part + 1) * RUN, :], k_terms[r])
             if part == ROUNDS_PER_CHUNK - 1:
                 store_chunk(out_k, k_staged[n], n)
-            if has_q:
-                q_terms = prod_pool.tile([P, H, 1, 2, D], F32)
-                for h in range(H):
-                    table_products(q_terms[:, h, 0, :, :], products[r, "q"], h, rstds[r, "q"], q_tables[b][:, 0, :, :])
+            if r % (CHUNKS * ROUNDS_PER_CHUNK) == 0:
                 q_staged = out_pool.tile([P, H, 1, D], F32)
-                add_swapped(q_staged, q_terms)
-                nc.sync.dma_start(out=out_q[b].rearrange("h p d -> p h d"), in_=q_staged[:, :, 0, :])
+                add_swapped(q_staged, q_terms[r])
+                nc.sync.dma_start(out=out_q[n // CHUNKS].rearrange("h p d -> p h d"), in_=q_staged[:, :, 0, :])
 
-        stages = (flip_round, quantise_round, project_round, rotate_round)
+        def prepare(n):
+            b, c = divmod(n, CHUNKS)
+            if n + PREFETCH < N_CHUNKS:
+                x_chunks[n + PREFETCH] = load_chunk(n + PREFETCH)
+            if c == 0 and b + 1 < B:
+                angles[b + 1] = (load_angles(cos, b + 1, "cos_sb"), load_angles(sin, b + 1, "sin_sb"))
+            if n + AHEAD < N_CHUNKS:
+                build_tables(n + AHEAD)
+
+        stages = (flip_round, quantise_round, project_round, multiply_round, add_round)
         for step in range(N_ROUNDS + len(stages) - 1):
             for lag, stage in enumerate(stages):
                 if 0 <= step - lag < N_ROUNDS:
                     stage(step - lag)
+            if step % ROUNDS_PER_CHUNK == 0 and step < N_ROUNDS:
+                prepare(step // ROUNDS_PER_CHUNK)
 
 
 def context_range(c):

@@ -23,7 +23,8 @@ K_PASS = 512
 PASSES = HID // K_PASS
 ROW_WORDS = HID // 2
 ROW_CODES = HID // 4
-N_OUT = 512
+HEADS = 4
+BANK = 512
 
 CTX_ROWS = CTX // P
 TILES = CTX_ROWS + 1
@@ -47,11 +48,11 @@ def tile_dflashattention_pa_t_kernel(
         angle_pool = stack.enter_context(tc.tile_pool(name="angles", bufs=2))
         table_pool = stack.enter_context(tc.tile_pool(name="tables", bufs=AHEAD + 2))
         quant_pool = stack.enter_context(tc.tile_pool(name="quant", bufs=3))
-        stat_pool = stack.enter_context(tc.tile_pool(name="stats", bufs=3 * RUN))
+        stat_pool = stack.enter_context(tc.tile_pool(name="stats", bufs=4))
         prod_pool = stack.enter_context(tc.tile_pool(name="products", bufs=2))
         out_pool = stack.enter_context(tc.tile_pool(name="staged", bufs=3))
         flip_psum = stack.enter_context(tc.psum_pool(name="flip", bufs=3))
-        kv_psum = stack.enter_context(tc.psum_pool(name="kv", bufs=2 * RUN))
+        kv_psum = stack.enter_context(tc.psum_pool(name="kv", bufs=2))
         q_psum = stack.enter_context(tc.psum_pool(name="q", bufs=1))
         stack.enter_context(tc.manual_schedule())
 
@@ -101,33 +102,33 @@ def tile_dflashattention_pa_t_kernel(
             low, high = slice(0, HALF), slice(HALF, D)
 
             def weighted(out, angle, w):
-                nc.vector.tensor_tensor(out=out, in0=angle, in1=w.unsqueeze(1).to_broadcast(out.shape), op=ALU.mult)
+                nc.gpsimd.tensor_tensor(out=out, in0=angle, in1=w.unsqueeze(1).to_broadcast(out.shape), op=ALU.mult)
 
             weighted(table[:, :, 0, :], cos_sb[:, tiles, :], w_rows[:])
             weighted(table[:, :, 1, low], sin_sb[:, tiles, high], w_rows[:, low])
             weighted(table[:, :, 1, high], sin_sb[:, tiles, low], w_rows[:, high])
             return table
 
-        def sum_squares(product, heads, tag):
-            sumsq = stat_pool.tile([P, heads], F32, name="sumsq", tag="sumsq" + tag)
-            squares = stat_pool.tile([P, heads * D], BF16, name="squares", tag="squares" + tag)
-            for h in range(heads):
-                cols = slice(h * D, (h + 1) * D)
+        def sum_squares(product):
+            sumsq = stat_pool.tile([P, HEADS], F32)
+            squares = stat_pool.tile([P, BANK], BF16)
+            for i in range(HEADS):
+                cols = slice(i * D, (i + 1) * D)
                 nc.scalar.activation(
-                    out=squares[:, cols], in_=product[:, cols], func=ACT.Square, accum_out=sumsq[:, h : h + 1]
+                    out=squares[:, cols], in_=product[:, cols], func=ACT.Square, accum_out=sumsq[:, i : i + 1]
                 )
             return sumsq
 
-        def inverse_rms(sumsq, heads, tag):
-            rstd = stat_pool.tile([P, heads], F32, name="rstd", tag="rstd" + tag)
+        def inverse_rms(sumsq):
+            rstd = stat_pool.tile([P, HEADS], F32)
             nc.scalar.activation(out=rstd[:], in_=sumsq[:], func=ACT.Abs_reciprocal_sqrt, scale=1.0 / D, bias=EPS)
             return rstd
 
-        def table_products(terms, product, h, rstd, table):
+        def table_products(terms, product, i, rstd, table):
             nc.vector.scalar_tensor_tensor(
                 out=terms,
-                in0=product[:, h * D : (h + 1) * D].unsqueeze(1).to_broadcast([P, 2, D]),
-                scalar=rstd[:, h : h + 1],
+                in0=product[:, i * D : (i + 1) * D].unsqueeze(1).to_broadcast([P, 2, D]),
+                scalar=rstd[:, i : i + 1],
                 in1=table,
                 op0=ALU.mult,
                 op1=ALU.mult,
@@ -153,12 +154,12 @@ def tile_dflashattention_pa_t_kernel(
 
         w_heads = [Wk[0:P, :], Wk[P : 2 * P, :], Wv[0:P, :], Wv[P : 2 * P, :]]
         w_heads.extend(Wq[h * P : (h + 1) * P, :] for h in range(H))
-        angles = {0: (load_angles(cos, 0, "cos_sb"), load_angles(sin, 0, "sin_sb"))}
         w_raw = const.tile([P, len(w_heads) * HID], BF16)
         for i, rows in enumerate(w_heads):
             nc.sync.dma_start(out=w_raw[:, i * HID : (i + 1) * HID], in_=rows)
-        x_chunks = {}
-        for n in range(PREFETCH):
+        x_chunks = {0: load_chunk(0)}
+        angles = {0: (load_angles(cos, 0, "cos_sb"), load_angles(sin, 0, "sin_sb"))}
+        for n in range(1, PREFETCH):
             x_chunks[n] = load_chunk(n)
 
         tables, q_tables = {}, {}
@@ -175,24 +176,26 @@ def tile_dflashattention_pa_t_kernel(
 
         w_codes, w_scales = {}, {}
         for block, name in enumerate(("kv", "q")):
-            w_grouped = const.tile([P, PASSES * N_OUT * 4], BF16, name="w_grouped_" + name, align_bytes=64)
+            w_grouped = const.tile([P, PASSES * BANK * 4], BF16, name="w_grouped_" + name, align_bytes=64)
             grouped_words = w_grouped[:].bitcast(F32).rearrange("p (g n u) -> p g n u", g=PASSES, u=2)
-            for i in range(N_OUT // P):
-                head = block * (N_OUT // P) + i
+            for i in range(BANK // P):
+                head = block * (BANK // P) + i
                 flipped = flip_rows(w_raw[:, head * HID : (head + 1) * HID].bitcast(F32))
-                copy_grouped(nc.scalar.copy, grouped_words[:, :, i * P : (i + 1) * P, :], flipped)
-            w_codes[name] = const.tile([P, PASSES * N_OUT], U32, name="w_codes_" + name, align_bytes=64)
-            w_scales[name] = const.tile([P, PASSES * N_OUT], U8, name="w_scales_" + name, align_bytes=64)
+                copy = nc.scalar.copy if i % 2 == 0 else nc.vector.tensor_copy
+                copy_grouped(copy, grouped_words[:, :, i * P : (i + 1) * P, :], flipped)
+            w_codes[name] = const.tile([P, PASSES * BANK], U32, name="w_codes_" + name, align_bytes=64)
+            w_scales[name] = const.tile([P, PASSES * BANK], U8, name="w_scales_" + name, align_bytes=64)
             nc.vector.quantize_mx(out=w_codes[name][:].bitcast(FP8X4), scales=w_scales[name][:], in_=w_grouped[:])
 
-        grouped, codes, scales, k_terms, q_terms = {}, {}, {}, {}, {}
+        grouped, codes, scales = {}, {}, {}
         products, rstds = {}, {}
-        k_staged, v_staged = {}, {}
+        k_terms, v_staged = {}, {}
+        q_terms = {}
 
-        def project(out, r, t, name):
+        def project(out, r, t, name, first, width):
             for g in range(PASSES):
                 x_cols = slice(t * ROW_CODES + g * P, t * ROW_CODES + (g + 1) * P)
-                w_cols = slice(g * N_OUT, (g + 1) * N_OUT)
+                w_cols = slice(g * BANK + first, g * BANK + first + width)
                 nc.tensor.matmul_mx(
                     out=out,
                     lhsT=codes[r][:, x_cols].bitcast(FP8X4),
@@ -223,49 +226,58 @@ def tile_dflashattention_pa_t_kernel(
         def project_round(r):
             n, part = divmod(r, ROUNDS_PER_CHUNK)
             has_q = r % (CHUNKS * ROUNDS_PER_CHUNK) == 0
+            width = KVH * D
+            for name in ("k", "v"):
+                products[r, name] = kv_psum.tile([P, BANK], F32, name=name + "_product")
+            for t in range(RUN):
+                project(products[r, "k"][:, t * width : (t + 1) * width], r, t, "kv", 0, width)
+                project(products[r, "v"][:, t * width : (t + 1) * width], r, t, "kv", width, width)
+            if has_q:
+                products[r, "q"] = q_psum.tile([P, BANK], F32, name="q_product")
+                project(products[r, "q"][:], r, 0, "q", 0, BANK)
+            k_sumsq = sum_squares(products[r, "k"])
+            if has_q:
+                q_sumsq = sum_squares(products[r, "q"])
             if part == 0:
-                k_staged[n] = out_pool.tile([P, KVH, CHUNK, D], F32, name="k_staged")
                 v_staged[n] = out_pool.tile([P, KVH, CHUNK, D], F32, name="v_staged")
-            for t in range(RUN):
-                products[r, t] = kv_psum.tile([P, N_OUT], F32, name="kv_product")
-                project(products[r, t][:], r, t, "kv")
-                if has_q and t == 0:
-                    products[r, "q"] = q_psum.tile([P, N_OUT], F32, name="q_product")
-                    project(products[r, "q"][:], r, t, "q")
-            for t in range(RUN):
-                k_sumsq = sum_squares(products[r, t], KVH, "k")
-                if has_q and t == 0:
-                    q_sumsq = sum_squares(products[r, "q"], H, "q")
-                nc.scalar.copy(
-                    out=v_staged[n][:, :, part * RUN + t, :],
-                    in_=products[r, t][:, KVH * D :].rearrange("p (h d) -> p h d", h=KVH),
-                )
-                rstds[r, t] = inverse_rms(k_sumsq, KVH, "k")
-                if has_q and t == 0:
-                    rstds[r, "q"] = inverse_rms(q_sumsq, H, "q")
+            nc.scalar.copy(
+                out=v_staged[n][:, :, part * RUN : (part + 1) * RUN, :].rearrange("p h t d -> p t h d"),
+                in_=products[r, "v"][:].rearrange("p (t h d) -> p t h d", t=RUN, h=KVH),
+            )
+            rstds[r, "k"] = inverse_rms(k_sumsq)
+            if has_q:
+                rstds[r, "q"] = inverse_rms(q_sumsq)
             if part == ROUNDS_PER_CHUNK - 1:
                 store_chunk(out_v, v_staged[n], n)
 
         def multiply_round(r):
             n, part = divmod(r, ROUNDS_PER_CHUNK)
-            k_terms[r] = prod_pool.tile([P, KVH, RUN, 2, D], F32, name="k_terms")
+            if part == 0:
+                k_terms[n] = prod_pool.tile([P, CHUNK, KVH, 2, D], F32, name="k_terms")
             for t in range(RUN):
+                tile = part * RUN + t
                 for h in range(KVH):
-                    table_products(k_terms[r][:, h, t, :, :], products[r, t], h, rstds[r, t], tables[n][:, part * RUN + t, :, :])
+                    table_products(
+                        k_terms[n][:, tile, h, :, :], products[r, "k"], t * KVH + h, rstds[r, "k"], tables[n][:, tile, :, :]
+                    )
             if r % (CHUNKS * ROUNDS_PER_CHUNK) == 0:
-                q_terms[r] = prod_pool.tile([P, H, 1, 2, D], F32, name="q_terms")
+                b = n // CHUNKS
+                q_terms[b] = prod_pool.tile([P, 1, H, 2, D], F32, name="q_terms")
                 for h in range(H):
-                    table_products(q_terms[r][:, h, 0, :, :], products[r, "q"], h, rstds[r, "q"], q_tables[n // CHUNKS][:, 0, :, :])
+                    table_products(q_terms[b][:, 0, h, :, :], products[r, "q"], h, rstds[r, "q"], q_tables[b][:, 0, :, :])
 
         def add_round(r):
             n, part = divmod(r, ROUNDS_PER_CHUNK)
-            add_swapped(k_staged[n][:, :, part * RUN : (part + 1) * RUN, :], k_terms[r])
-            if part == ROUNDS_PER_CHUNK - 1:
-                store_chunk(out_k, k_staged[n], n)
-            if r % (CHUNKS * ROUNDS_PER_CHUNK) == 0:
+            b, c = divmod(n, CHUNKS)
+            if part != ROUNDS_PER_CHUNK - 1:
+                return
+            k_staged = out_pool.tile([P, KVH, CHUNK, D], F32)
+            add_swapped(k_staged[:].rearrange("p h t d -> p t h d"), k_terms[n])
+            store_chunk(out_k, k_staged, n)
+            if c == 0:
                 q_staged = out_pool.tile([P, H, 1, D], F32)
-                add_swapped(q_staged, q_terms[r])
-                nc.sync.dma_start(out=out_q[n // CHUNKS].rearrange("h p d -> p h d"), in_=q_staged[:, :, 0, :])
+                add_swapped(q_staged[:].rearrange("p h t d -> p t h d"), q_terms[b])
+                nc.sync.dma_start(out=out_q[b].rearrange("h p d -> p h d"), in_=q_staged[:, :, 0, :])
 
         def prepare(n):
             b, c = divmod(n, CHUNKS)

@@ -62,10 +62,17 @@ def tile_dflashattention_pa_t_kernel(
         nc.vector.memset(one[:], 1.0)
         warm = const.tile([P, 1], F32)
         nc.scalar.activation(out=warm[:], in_=one[:], func=ACT.Abs_reciprocal_sqrt)
-        wk_rows = const.tile([P, D], BF16)
-        nc.scalar.dma_start(out=wk_rows[:], in_=k_norm_w.partition_broadcast(P))
-        wq_rows = const.tile([P, D], BF16)
-        nc.scalar.dma_start(out=wq_rows[:], in_=q_norm_w.partition_broadcast(P))
+        w_first_row = const.tile([P, 2 * D], BF16)
+        nc.vector.memset(w_first_row[:], 0.0)
+        nc.scalar.dma_start(out=w_first_row[0:1, 0:D], in_=k_norm_w.unsqueeze(0))
+        nc.scalar.dma_start(out=w_first_row[0:1, D : 2 * D], in_=q_norm_w.unsqueeze(0))
+        ones = const.tile([P, P], BF16)
+        nc.vector.memset(ones[:], 1.0)
+        w_spread = flip_psum.tile([P, 2 * D], F32, tag="flipped")
+        nc.tensor.matmul(out=w_spread[:], lhsT=ones[:], rhs=w_first_row[:], start=True, stop=True)
+        w_all_rows = const.tile([P, 2 * D], F32)
+        nc.vector.tensor_copy(out=w_all_rows[:], in_=w_spread[:])
+        wk_rows, wq_rows = w_all_rows[:, 0:D], w_all_rows[:, D : 2 * D]
 
         def flip_rows(words):
             flipped = flip_psum.tile([P, PASSES, 2, P], F32)
@@ -104,7 +111,7 @@ def tile_dflashattention_pa_t_kernel(
             def weighted(out, angle, w):
                 nc.gpsimd.tensor_tensor(out=out, in0=angle, in1=w.unsqueeze(1).to_broadcast(out.shape), op=ALU.mult)
 
-            weighted(table[:, :, 0, :], cos_sb[:, tiles, :], w_rows[:])
+            weighted(table[:, :, 0, :], cos_sb[:, tiles, :], w_rows)
             weighted(table[:, :, 1, low], sin_sb[:, tiles, high], w_rows[:, low])
             weighted(table[:, :, 1, high], sin_sb[:, tiles, low], w_rows[:, high])
             return table

@@ -68,11 +68,6 @@ def tile_dflashattention_pa_t_kernel(
         nc.scalar.dma_start(out=w_first_row[0:1, D : 2 * D], in_=q_norm_w.unsqueeze(0))
         ones = const.tile([P, P], BF16)
         nc.vector.memset(ones[:], 1.0)
-        w_spread = flip_psum.tile([P, 2 * D], F32, tag="flipped")
-        nc.tensor.matmul(out=w_spread[:], lhsT=ones[:], rhs=w_first_row[:], start=True, stop=True)
-        w_all_rows = const.tile([P, 2 * D], F32)
-        nc.vector.tensor_copy(out=w_all_rows[:], in_=w_spread[:])
-        wk_rows, wq_rows = w_all_rows[:, 0:D], w_all_rows[:, D : 2 * D]
 
         def flip_rows(words):
             flipped = flip_psum.tile([P, PASSES, 2, P], F32)
@@ -169,18 +164,6 @@ def tile_dflashattention_pa_t_kernel(
         for n in range(1, PREFETCH):
             x_chunks[n] = load_chunk(n)
 
-        tables, q_tables = {}, {}
-
-        def build_tables(n):
-            b, c = divmod(n, CHUNKS)
-            cos_sb, sin_sb = angles[b]
-            tables[n] = rope_table(cos_sb, sin_sb, c * CHUNK, CHUNK, wk_rows, "k")
-            if c == 0:
-                q_tables[b] = rope_table(cos_sb, sin_sb, 0, 1, wq_rows, "q")
-
-        for n in range(AHEAD):
-            build_tables(n)
-
         w_codes, w_scales = {}, {}
         for block, name in enumerate(("kv", "q")):
             w_grouped = const.tile([P, PASSES * BANK * 4], BF16, name="w_grouped_" + name, align_bytes=64)
@@ -193,6 +176,24 @@ def tile_dflashattention_pa_t_kernel(
             w_codes[name] = const.tile([P, PASSES * BANK], U32, name="w_codes_" + name, align_bytes=64)
             w_scales[name] = const.tile([P, PASSES * BANK], U8, name="w_scales_" + name, align_bytes=64)
             nc.vector.quantize_mx(out=w_codes[name][:].bitcast(FP8X4), scales=w_scales[name][:], in_=w_grouped[:])
+
+        w_spread = flip_psum.tile([P, 2 * D], F32, tag="flipped")
+        nc.tensor.matmul(out=w_spread[:], lhsT=ones[:], rhs=w_first_row[:], start=True, stop=True)
+        w_all_rows = const.tile([P, 2 * D], F32)
+        nc.vector.tensor_copy(out=w_all_rows[:], in_=w_spread[:])
+        wk_rows, wq_rows = w_all_rows[:, 0:D], w_all_rows[:, D : 2 * D]
+
+        tables, q_tables = {}, {}
+
+        def build_tables(n):
+            b, c = divmod(n, CHUNKS)
+            cos_sb, sin_sb = angles[b]
+            tables[n] = rope_table(cos_sb, sin_sb, c * CHUNK, CHUNK, wk_rows, "k")
+            if c == 0:
+                q_tables[b] = rope_table(cos_sb, sin_sb, 0, 1, wq_rows, "q")
+
+        for n in range(AHEAD):
+            build_tables(n)
 
         grouped, codes, scales = {}, {}, {}
         products, rstds = {}, {}
@@ -213,35 +214,34 @@ def tile_dflashattention_pa_t_kernel(
                     stop=(g == PASSES - 1),
                 )
 
-        def flip_round(r):
+        def flip_tile(r, t):
             n, part = divmod(r, ROUNDS_PER_CHUNK)
-            grouped[r] = quant_pool.tile([P, RUN * HID], BF16, name="grouped", align_bytes=64)
-            words = x_chunks[n][:].bitcast(F32)
-            flipped = [
-                flip_rows(words[:, (part * RUN + t) * ROW_WORDS : (part * RUN + t + 1) * ROW_WORDS])
-                for t in range(RUN)
-            ]
-            for t in range(RUN):
-                tile_words = grouped[r][:, t * HID : (t + 1) * HID].bitcast(F32)
-                copy_grouped(nc.scalar.copy, tile_words.rearrange("p (g r u) -> p g r u", g=PASSES, u=2), flipped[t])
+            if t == 0:
+                grouped[r] = quant_pool.tile([P, RUN * HID], BF16, name="grouped", align_bytes=64)
+            tile = part * RUN + t
+            flipped = flip_rows(x_chunks[n][:, tile * HID : (tile + 1) * HID].bitcast(F32))
+            tile_words = grouped[r][:, t * HID : (t + 1) * HID].bitcast(F32)
+            copy_grouped(nc.scalar.copy, tile_words.rearrange("p (g r u) -> p g r u", g=PASSES, u=2), flipped)
 
         def quantise_round(r):
             codes[r] = quant_pool.tile([P, RUN * ROW_CODES], U32, name="codes", align_bytes=64)
             scales[r] = quant_pool.tile([P, RUN * ROW_CODES], U8, name="scales", align_bytes=64)
             nc.vector.quantize_mx(out=codes[r][:].bitcast(FP8X4), scales=scales[r][:], in_=grouped[r][:])
 
-        def project_round(r):
-            n, part = divmod(r, ROUNDS_PER_CHUNK)
-            has_q = r % (CHUNKS * ROUNDS_PER_CHUNK) == 0
+        def project_tile(r, t):
             width = KVH * D
-            for name in ("k", "v"):
-                products[r, name] = kv_psum.tile([P, BANK], F32, name=name + "_product")
-            for t in range(RUN):
-                project(products[r, "k"][:, t * width : (t + 1) * width], r, t, "kv", 0, width)
-                project(products[r, "v"][:, t * width : (t + 1) * width], r, t, "kv", width, width)
-            if has_q:
+            if t == 0:
+                for name in ("k", "v"):
+                    products[r, name] = kv_psum.tile([P, BANK], F32, name=name + "_product")
+            project(products[r, "k"][:, t * width : (t + 1) * width], r, t, "kv", 0, width)
+            project(products[r, "v"][:, t * width : (t + 1) * width], r, t, "kv", width, width)
+            if t == 0 and r % (CHUNKS * ROUNDS_PER_CHUNK) == 0:
                 products[r, "q"] = q_psum.tile([P, BANK], F32, name="q_product")
                 project(products[r, "q"][:], r, 0, "q", 0, BANK)
+
+        def norm_round(r):
+            n, part = divmod(r, ROUNDS_PER_CHUNK)
+            has_q = r % (CHUNKS * ROUNDS_PER_CHUNK) == 0
             k_sumsq = sum_squares(products[r, "k"])
             if has_q:
                 q_sumsq = sum_squares(products[r, "q"])
@@ -295,9 +295,14 @@ def tile_dflashattention_pa_t_kernel(
             if n + AHEAD < N_CHUNKS:
                 build_tables(n + AHEAD)
 
-        stages = (flip_round, quantise_round, project_round, multiply_round, add_round)
-        for step in range(N_ROUNDS + len(stages) - 1):
-            for lag, stage in enumerate(stages):
+        later_stages = (quantise_round, norm_round, multiply_round, add_round)
+        for step in range(N_ROUNDS + len(later_stages)):
+            for t in range(RUN):
+                if step < N_ROUNDS:
+                    flip_tile(step, t)
+                if 0 <= step - 2 < N_ROUNDS:
+                    project_tile(step - 2, t)
+            for lag, stage in enumerate(later_stages, 1):
                 if 0 <= step - lag < N_ROUNDS:
                     stage(step - lag)
             if step % ROUNDS_PER_CHUNK == 0 and step < N_ROUNDS:

@@ -52,8 +52,8 @@ def tile_dflashattention_pa_t_kernel(
         prod_pool = stack.enter_context(tc.tile_pool(name="products", bufs=2))
         out_pool = stack.enter_context(tc.tile_pool(name="staged", bufs=3))
         flip_psum = stack.enter_context(tc.psum_pool(name="flip", bufs=3))
-        kv_psum = stack.enter_context(tc.psum_pool(name="kv", bufs=2))
-        q_psum = stack.enter_context(tc.psum_pool(name="q", bufs=1))
+        head_psum = stack.enter_context(tc.psum_pool(name="heads", bufs=3))
+        v_psum = stack.enter_context(tc.psum_pool(name="v", bufs=2))
         stack.enter_context(tc.manual_schedule())
 
         identity = const.tile([P, P], F32)
@@ -214,30 +214,34 @@ def tile_dflashattention_pa_t_kernel(
                     stop=(g == PASSES - 1),
                 )
 
-        def flip_tile(r, t):
+        def flip_round(r):
             n, part = divmod(r, ROUNDS_PER_CHUNK)
-            if t == 0:
-                grouped[r] = quant_pool.tile([P, RUN * HID], BF16, name="grouped", align_bytes=64)
-            tile = part * RUN + t
-            flipped = flip_rows(x_chunks[n][:, tile * HID : (tile + 1) * HID].bitcast(F32))
-            tile_words = grouped[r][:, t * HID : (t + 1) * HID].bitcast(F32)
-            copy_grouped(nc.scalar.copy, tile_words.rearrange("p (g r u) -> p g r u", g=PASSES, u=2), flipped)
+            grouped[r] = quant_pool.tile([P, RUN * HID], BF16, name="grouped", align_bytes=64)
+            words = x_chunks[n][:].bitcast(F32)
+            flipped = [
+                flip_rows(words[:, (part * RUN + t) * ROW_WORDS : (part * RUN + t + 1) * ROW_WORDS])
+                for t in range(RUN)
+            ]
+            for t in range(RUN):
+                tile_words = grouped[r][:, t * HID : (t + 1) * HID].bitcast(F32)
+                copy_grouped(nc.scalar.copy, tile_words.rearrange("p (g r u) -> p g r u", g=PASSES, u=2), flipped[t])
 
         def quantise_round(r):
             codes[r] = quant_pool.tile([P, RUN * ROW_CODES], U32, name="codes", align_bytes=64)
             scales[r] = quant_pool.tile([P, RUN * ROW_CODES], U8, name="scales", align_bytes=64)
             nc.vector.quantize_mx(out=codes[r][:].bitcast(FP8X4), scales=scales[r][:], in_=grouped[r][:])
 
-        def project_tile(r, t):
+        def project_round(r):
             width = KVH * D
-            if t == 0:
-                for name in ("k", "v"):
-                    products[r, name] = kv_psum.tile([P, BANK], F32, name=name + "_product")
-            project(products[r, "k"][:, t * width : (t + 1) * width], r, t, "kv", 0, width)
-            project(products[r, "v"][:, t * width : (t + 1) * width], r, t, "kv", width, width)
-            if t == 0 and r % (CHUNKS * ROUNDS_PER_CHUNK) == 0:
-                products[r, "q"] = q_psum.tile([P, BANK], F32, name="q_product")
+            products[r, "k"] = head_psum.tile([P, BANK], F32, name="head_product")
+            for t in range(RUN):
+                project(products[r, "k"][:, t * width : (t + 1) * width], r, t, "kv", 0, width)
+            if r % (CHUNKS * ROUNDS_PER_CHUNK) == 0:
+                products[r, "q"] = head_psum.tile([P, BANK], F32, name="head_product")
                 project(products[r, "q"][:], r, 0, "q", 0, BANK)
+            products[r, "v"] = v_psum.tile([P, BANK], F32, name="v_product")
+            for t in range(RUN):
+                project(products[r, "v"][:, t * width : (t + 1) * width], r, t, "kv", width, width)
 
         def norm_round(r):
             n, part = divmod(r, ROUNDS_PER_CHUNK)
@@ -295,14 +299,9 @@ def tile_dflashattention_pa_t_kernel(
             if n + AHEAD < N_CHUNKS:
                 build_tables(n + AHEAD)
 
-        later_stages = (quantise_round, norm_round, multiply_round, add_round)
-        for step in range(N_ROUNDS + len(later_stages)):
-            for t in range(RUN):
-                if step < N_ROUNDS:
-                    flip_tile(step, t)
-                if 0 <= step - 2 < N_ROUNDS:
-                    project_tile(step - 2, t)
-            for lag, stage in enumerate(later_stages, 1):
+        stages = ((0, flip_round), (1, quantise_round), (2, project_round), (2, norm_round), (3, multiply_round), (4, add_round))
+        for step in range(N_ROUNDS + 4):
+            for lag, stage in stages:
                 if 0 <= step - lag < N_ROUNDS:
                     stage(step - lag)
             if step % ROUNDS_PER_CHUNK == 0 and step < N_ROUNDS:

@@ -54,7 +54,6 @@ def tile_dflashattention_pa_t_kernel(
         flip_psum = stack.enter_context(tc.psum_pool(name="flip", bufs=3))
         head_psum = stack.enter_context(tc.psum_pool(name="heads", bufs=3))
         v_psum = stack.enter_context(tc.psum_pool(name="v", bufs=2))
-        stack.enter_context(tc.manual_schedule())
 
         identity = const.tile([P, P], F32)
         make_identity(nc, identity[:])

@@ -54,6 +54,7 @@ def tile_dflashattention_pa_t_kernel(
         flip_psum = stack.enter_context(tc.psum_pool(name="flip", bufs=3))
         head_psum = stack.enter_context(tc.psum_pool(name="heads", bufs=3))
         v_psum = stack.enter_context(tc.psum_pool(name="v", bufs=2))
+        stack.enter_context(tc.manual_schedule())
 
         identity = const.tile([P, P], F32)
         make_identity(nc, identity[:])
@@ -135,12 +136,12 @@ def tile_dflashattention_pa_t_kernel(
                 op1=ALU.mult,
             )
 
-        def add_swapped(staged, terms):
-            nc.vector.tensor_tensor(
+        def add_swapped(engine, staged, terms):
+            engine.tensor_tensor(
                 out=staged[:, :, :, 0:HALF], in0=terms[:, :, :, 0, 0:HALF], in1=terms[:, :, :, 1, HALF:D],
                 op=ALU.subtract,
             )
-            nc.vector.tensor_tensor(
+            engine.tensor_tensor(
                 out=staged[:, :, :, HALF:D], in0=terms[:, :, :, 0, HALF:D], in1=terms[:, :, :, 1, 0:HALF],
                 op=ALU.add,
             )
@@ -282,11 +283,11 @@ def tile_dflashattention_pa_t_kernel(
             if part != ROUNDS_PER_CHUNK - 1:
                 return
             k_staged = out_pool.tile([P, KVH, CHUNK, D], F32)
-            add_swapped(k_staged[:].rearrange("p h t d -> p t h d"), k_terms[n])
+            add_swapped(nc.vector, k_staged[:].rearrange("p h t d -> p t h d"), k_terms[n])
             store_chunk(out_k, k_staged, n)
             if c == 0:
                 q_staged = out_pool.tile([P, H, 1, D], F32)
-                add_swapped(q_staged[:].rearrange("p h t d -> p t h d"), q_terms[b])
+                add_swapped(nc.gpsimd, q_staged[:].rearrange("p h t d -> p t h d"), q_terms[b])
                 nc.sync.dma_start(out=out_q[b].rearrange("h p d -> p h d"), in_=q_staged[:, :, 0, :])
 
         def prepare(n):

from contextlib import ExitStack

import concourse.mybir as mybir
from concourse.masks import make_identity

FP8X4 = mybir.dt.float8_e4m3fn_x4
BF16 = mybir.dt.bfloat16
F32 = mybir.dt.float32
U32 = mybir.dt.uint32
U8 = mybir.dt.uint8
ACT = mybir.ActivationFunctionType
ALU = mybir.AluOpType

P = 128
B, Q_LEN, CTX, HID, H, KVH, D = 4, 128, 1408, 1024, 4, 2, 128
T = CTX + Q_LEN
EPS = 1e-6
HALF = D // 2

FLOPS = 2 * HID * (B * T * 2 * KVH * D + B * Q_LEN * H * D)

K_PASS = 512
PASSES = HID // K_PASS
ROW_WORDS = HID // 2
ROW_CODES = HID // 4
HEADS = 4
BANK = 512

CTX_ROWS = CTX // P
TILES = CTX_ROWS + 1
CHUNK = 4
CHUNKS = TILES // CHUNK
RUN = 2
N_CHUNKS = B * CHUNKS
ROUNDS_PER_CHUNK = CHUNK // RUN
N_ROUNDS = N_CHUNKS * ROUNDS_PER_CHUNK
PREFETCH = 5
AHEAD = 2


def tile_dflashattention_pa_t_kernel(
    tc, hidden_states, target_hidden, cos, sin, Wq, Wk, Wv, q_norm_w, k_norm_w, out_q, out_k, out_v
):
    nc = tc.nc
    with ExitStack() as stack:
        const = stack.enter_context(tc.tile_pool(name="const", bufs=1))
        x_pool = stack.enter_context(tc.tile_pool(name="x", bufs=PREFETCH + 1))
        angle_pool = stack.enter_context(tc.tile_pool(name="angles", bufs=2))
        table_pool = stack.enter_context(tc.tile_pool(name="tables", bufs=AHEAD + 2))
        quant_pool = stack.enter_context(tc.tile_pool(name="quant", bufs=3))
        stat_pool = stack.enter_context(tc.tile_pool(name="stats", bufs=4))
        prod_pool = stack.enter_context(tc.tile_pool(name="products", bufs=2))
        out_pool = stack.enter_context(tc.tile_pool(name="staged", bufs=3))
        flip_psum = stack.enter_context(tc.psum_pool(name="flip", bufs=3))
        head_psum = stack.enter_context(tc.psum_pool(name="heads", bufs=3))
        v_psum = stack.enter_context(tc.psum_pool(name="v", bufs=2))
        stack.enter_context(tc.manual_schedule())

        identity = const.tile([P, P], F32)
        make_identity(nc, identity[:])
        one = const.tile([P, 1], F32)
        nc.vector.memset(one[:], 1.0)
        warm = const.tile([P, 1], F32)
        nc.scalar.activation(out=warm[:], in_=one[:], func=ACT.Abs_reciprocal_sqrt)
        w_first_row = const.tile([P, 2 * D], BF16)
        nc.vector.memset(w_first_row[:], 0.0)
        nc.scalar.dma_start(out=w_first_row[0:1, 0:D], in_=k_norm_w.unsqueeze(0))
        nc.scalar.dma_start(out=w_first_row[0:1, D : 2 * D], in_=q_norm_w.unsqueeze(0))
        ones = const.tile([P, P], BF16)
        nc.vector.memset(ones[:], 1.0)

        def flip_rows(words):
            flipped = flip_psum.tile([P, PASSES, 2, P], F32)
            for g in range(PASSES):
                for u in range(2):
                    first = (2 * g + u) * P
                    nc.tensor.transpose(flipped[:, g, u, :], words[:, first : first + P], identity[:])
            return flipped

        def copy_grouped(copy, grouped_words, flipped):
            copy(out=grouped_words, in_=flipped[:].rearrange("p g u r -> p g r u"))

        def load_chunk(n):
            b, c = divmod(n, CHUNKS)
            x_sb = x_pool.tile([P, CHUNK * HID], BF16)
            local, first, last = context_range(c)
            if c == 0:
                nc.sync.dma_start(out=x_sb[:, 0:HID], in_=hidden_states[b])
            rows = target_hidden[b].rearrange("(p j) c -> p (j c)", j=CTX_ROWS)
            nc.sync.dma_start(out=x_sb[:, local * HID :], in_=rows[:, first * HID : last * HID])
            return x_sb

        def load_angles(table, b, tag):
            angle_sb = angle_pool.tile([P, TILES, D], BF16, name=tag)
            nc.sync.dma_start(out=angle_sb[:, 0, :], in_=table[b, CTX:T, :])
            nc.sync.dma_start(
                out=angle_sb[:, 1:TILES, :], in_=table[b, 0:CTX, :].rearrange("(p j) d -> p j d", j=CTX_ROWS)
            )
            return angle_sb

        def rope_table(cos_sb, sin_sb, first, count, w_rows, tag):
            table = table_pool.tile([P, count, 2, D], F32, name="table", tag=tag)
            tiles = slice(first, first + count)
            low, high = slice(0, HALF), slice(HALF, D)

            def weighted(out, angle, w):
                nc.gpsimd.tensor_tensor(out=out, in0=angle, in1=w.unsqueeze(1).to_broadcast(out.shape), op=ALU.mult)

            weighted(table[:, :, 0, :], cos_sb[:, tiles, :], w_rows)
            weighted(table[:, :, 1, low], sin_sb[:, tiles, high], w_rows[:, low])
            weighted(table[:, :, 1, high], sin_sb[:, tiles, low], w_rows[:, high])
            return table

        def sum_squares(product):
            sumsq = stat_pool.tile([P, HEADS], F32)
            squares = stat_pool.tile([P, BANK], BF16)
            for i in range(HEADS):
                cols = slice(i * D, (i + 1) * D)
                nc.scalar.activation(
                    out=squares[:, cols], in_=product[:, cols], func=ACT.Square, accum_out=sumsq[:, i : i + 1]
                )
            return sumsq

        def inverse_rms(sumsq):
            rstd = stat_pool.tile([P, HEADS], F32)
            nc.scalar.activation(out=rstd[:], in_=sumsq[:], func=ACT.Abs_reciprocal_sqrt, scale=1.0 / D, bias=EPS)
            return rstd

        def table_products(terms, product, i, rstd, table):
            nc.vector.scalar_tensor_tensor(
                out=terms,
                in0=product[:, i * D : (i + 1) * D].unsqueeze(1).to_broadcast([P, 2, D]),
                scalar=rstd[:, i : i + 1],
                in1=table,
                op0=ALU.mult,
                op1=ALU.mult,
            )

        def add_swapped(engine, staged, terms):
            engine.tensor_tensor(
                out=staged[:, :, :, 0:HALF], in0=terms[:, :, :, 0, 0:HALF], in1=terms[:, :, :, 1, HALF:D],
                op=ALU.subtract,
            )
            engine.tensor_tensor(
                out=staged[:, :, :, HALF:D], in0=terms[:, :, :, 0, HALF:D], in1=terms[:, :, :, 1, 0:HALF],
                op=ALU.add,
            )

        def store_chunk(dst, staged, n):
            b, c = divmod(n, CHUNKS)
            local, first, last = context_range(c)
            rows = dst[b, :, 0:CTX, :].rearrange("h (p j) d -> p h j d", j=CTX_ROWS)
            nc.sync.dma_start(out=rows[:, :, first:last, :], in_=staged[:, :, local:CHUNK, :])
            if c == 0:
                nc.sync.dma_start(out=dst[b, :, CTX:T, :].rearrange("h p d -> p h d"), in_=staged[:, :, 0, :])

        w_heads = [Wk[0:P, :], Wk[P : 2 * P, :], Wv[0:P, :], Wv[P : 2 * P, :]]
        w_heads.extend(Wq[h * P : (h + 1) * P, :] for h in range(H))
        w_raw = const.tile([P, len(w_heads) * HID], BF16)
        for i, rows in enumerate(w_heads):
            nc.sync.dma_start(out=w_raw[:, i * HID : (i + 1) * HID], in_=rows)
        x_chunks = {0: load_chunk(0)}
        angles = {0: (load_angles(cos, 0, "cos_sb"), load_angles(sin, 0, "sin_sb"))}
        for n in range(1, PREFETCH):
            x_chunks[n] = load_chunk(n)

        w_codes, w_scales = {}, {}
        for block, name in enumerate(("kv", "q")):
            w_grouped = const.tile([P, PASSES * BANK * 4], BF16, name="w_grouped_" + name, align_bytes=64)
            grouped_words = w_grouped[:].bitcast(F32).rearrange("p (g n u) -> p g n u", g=PASSES, u=2)
            for i in range(BANK // P):
                head = block * (BANK // P) + i
                flipped = flip_rows(w_raw[:, head * HID : (head + 1) * HID].bitcast(F32))
                copy = nc.scalar.copy if i % 2 == 0 else nc.vector.tensor_copy
                copy_grouped(copy, grouped_words[:, :, i * P : (i + 1) * P, :], flipped)
            w_codes[name] = const.tile([P, PASSES * BANK], U32, name="w_codes_" + name, align_bytes=64)
            w_scales[name] = const.tile([P, PASSES * BANK], U8, name="w_scales_" + name, align_bytes=64)
            nc.vector.quantize_mx(out=w_codes[name][:].bitcast(FP8X4), scales=w_scales[name][:], in_=w_grouped[:])

        w_spread = flip_psum.tile([P, 2 * D], F32, tag="flipped")
        nc.tensor.matmul(out=w_spread[:], lhsT=ones[:], rhs=w_first_row[:], start=True, stop=True)
        w_all_rows = const.tile([P, 2 * D], F32)
        nc.vector.tensor_copy(out=w_all_rows[:], in_=w_spread[:])
        wk_rows, wq_rows = w_all_rows[:, 0:D], w_all_rows[:, D : 2 * D]

        tables, q_tables = {}, {}

        def build_tables(n):
            b, c = divmod(n, CHUNKS)
            cos_sb, sin_sb = angles[b]
            tables[n] = rope_table(cos_sb, sin_sb, c * CHUNK, CHUNK, wk_rows, "k")
            if c == 0:
                q_tables[b] = rope_table(cos_sb, sin_sb, 0, 1, wq_rows, "q")

        for n in range(AHEAD):
            build_tables(n)

        grouped, codes, scales = {}, {}, {}
        products, rstds = {}, {}
        k_terms, v_staged = {}, {}
        q_terms = {}

        def project(out, r, t, name, first, width):
            for g in range(PASSES):
                x_cols = slice(t * ROW_CODES + g * P, t * ROW_CODES + (g + 1) * P)
                w_cols = slice(g * BANK + first, g * BANK + first + width)
                nc.tensor.matmul_mx(
                    out=out,
                    lhsT=codes[r][:, x_cols].bitcast(FP8X4),
                    lhsT_scale=scales[r][:, x_cols],
                    rhs=w_codes[name][:, w_cols].bitcast(FP8X4),
                    rhs_scale=w_scales[name][:, w_cols],
                    start=(g == 0),
                    stop=(g == PASSES - 1),
                )

        def flip_round(r):
            n, part = divmod(r, ROUNDS_PER_CHUNK)
            grouped[r] = quant_pool.tile([P, RUN * HID], BF16, name="grouped", align_bytes=64)
            words = x_chunks[n][:].bitcast(F32)
            flipped = [
                flip_rows(words[:, (part * RUN + t) * ROW_WORDS : (part * RUN + t + 1) * ROW_WORDS])
                for t in range(RUN)
            ]
            for t in range(RUN):
                tile_words = grouped[r][:, t * HID : (t + 1) * HID].bitcast(F32)
                copy_grouped(nc.scalar.copy, tile_words.rearrange("p (g r u) -> p g r u", g=PASSES, u=2), flipped[t])

        def quantise_round(r):
            codes[r] = quant_pool.tile([P, RUN * ROW_CODES], U32, name="codes", align_bytes=64)
            scales[r] = quant_pool.tile([P, RUN * ROW_CODES], U8, name="scales", align_bytes=64)
            nc.vector.quantize_mx(out=codes[r][:].bitcast(FP8X4), scales=scales[r][:], in_=grouped[r][:])

        def project_round(r):
            width = KVH * D
            products[r, "k"] = head_psum.tile([P, BANK], F32, name="head_product")
            for t in range(RUN):
                project(products[r, "k"][:, t * width : (t + 1) * width], r, t, "kv", 0, width)
            if r % (CHUNKS * ROUNDS_PER_CHUNK) == 0:
                products[r, "q"] = head_psum.tile([P, BANK], F32, name="head_product")
                project(products[r, "q"][:], r, 0, "q", 0, BANK)
            products[r, "v"] = v_psum.tile([P, BANK], F32, name="v_product")
            for t in range(RUN):
                project(products[r, "v"][:, t * width : (t + 1) * width], r, t, "kv", width, width)

        def norm_round(r):
            n, part = divmod(r, ROUNDS_PER_CHUNK)
            has_q = r % (CHUNKS * ROUNDS_PER_CHUNK) == 0
            k_sumsq = sum_squares(products[r, "k"])
            if has_q:
                q_sumsq = sum_squares(products[r, "q"])
            if part == 0:
                v_staged[n] = out_pool.tile([P, KVH, CHUNK, D], F32, name="v_staged")
            nc.scalar.copy(
                out=v_staged[n][:, :, part * RUN : (part + 1) * RUN, :].rearrange("p h t d -> p t h d"),
                in_=products[r, "v"][:].rearrange("p (t h d) -> p t h d", t=RUN, h=KVH),
            )
            rstds[r, "k"] = inverse_rms(k_sumsq)
            if has_q:
                rstds[r, "q"] = inverse_rms(q_sumsq)
            if part == ROUNDS_PER_CHUNK - 1:
                store_chunk(out_v, v_staged[n], n)

        def multiply_round(r):
            n, part = divmod(r, ROUNDS_PER_CHUNK)
            if part == 0:
                k_terms[n] = prod_pool.tile([P, CHUNK, KVH, 2, D], F32, name="k_terms")
            for t in range(RUN):
                tile = part * RUN + t
                for h in range(KVH):
                    table_products(
                        k_terms[n][:, tile, h, :, :], products[r, "k"], t * KVH + h, rstds[r, "k"], tables[n][:, tile, :, :]
                    )
            if r % (CHUNKS * ROUNDS_PER_CHUNK) == 0:
                b = n // CHUNKS
                q_terms[b] = prod_pool.tile([P, 1, H, 2, D], F32, name="q_terms")
                for h in range(H):
                    table_products(q_terms[b][:, 0, h, :, :], products[r, "q"], h, rstds[r, "q"], q_tables[b][:, 0, :, :])

        def add_round(r):
            n, part = divmod(r, ROUNDS_PER_CHUNK)
            b, c = divmod(n, CHUNKS)
            if part != ROUNDS_PER_CHUNK - 1:
                return
            k_staged = out_pool.tile([P, KVH, CHUNK, D], F32)
            add_swapped(nc.vector, k_staged[:].rearrange("p h t d -> p t h d"), k_terms[n])
            store_chunk(out_k, k_staged, n)
            if c == 0:
                q_staged = out_pool.tile([P, H, 1, D], F32)
                add_swapped(nc.gpsimd, q_staged[:].rearrange("p h t d -> p t h d"), q_terms[b])
                nc.sync.dma_start(out=out_q[b].rearrange("h p d -> p h d"), in_=q_staged[:, :, 0, :])

        def prepare(n):
            b, c = divmod(n, CHUNKS)
            if n + PREFETCH < N_CHUNKS:
                x_chunks[n + PREFETCH] = load_chunk(n + PREFETCH)
            if c == 0 and b + 1 < B:
                angles[b + 1] = (load_angles(cos, b + 1, "cos_sb"), load_angles(sin, b + 1, "sin_sb"))
            if n + AHEAD < N_CHUNKS:
                build_tables(n + AHEAD)

        stages = ((0, flip_round), (1, quantise_round), (2, project_round), (2, norm_round), (3, multiply_round), (4, add_round))
        for step in range(N_ROUNDS + 4):
            for lag, stage in stages:
                if 0 <= step - lag < N_ROUNDS:
                    stage(step - lag)
            if step % ROUNDS_PER_CHUNK == 0 and step < N_ROUNDS:
                prepare(step // ROUNDS_PER_CHUNK)


def context_range(c):
    local = 1 if c == 0 else 0
    first = c * CHUNK + local - 1
    return local, first, c * CHUNK + CHUNK - 1
